import numpy as np
import ml_dtypes


def mxq(x, axis, fmt="e4m3"):
    dtype, down = {"e4m3": (ml_dtypes.float8_e4m3fn, 7), "e5m2": (ml_dtypes.float8_e5m2, 14)}[fmt]
    v = np.moveaxis(np.asarray(x, np.float32).astype(ml_dtypes.bfloat16).astype(np.float64), axis, -1)
    blocks = v.reshape(v.shape[:-1] + (-1, 32))
    amax = np.abs(blocks).max(-1, keepdims=True)
    byte = np.maximum(np.where(amax > 0, np.frexp(amax)[1] - 1 + 127, 0) - down, 1)
    scale = np.exp2(byte - 127.0)
    codes = (blocks / scale).astype(np.float32).astype(dtype).astype(np.float64)
    return np.moveaxis((codes * scale).reshape(v.shape), -1, axis)


WIDE = False


def mx_kscale(k):
    if not WIDE:
        return np.ones(k)
    levels = np.array([10, -10, 5, -5, 0])
    if k % 512:
        return np.exp2(np.random.permutation(np.resize(levels, k // 32))).repeat(32)
    a = np.empty((k // 512, 16))
    for p in range(k // 512):
        a[p, :8] = np.random.permutation(np.resize(levels, 8))
        for g in range(8):
            far = levels[np.abs(levels - a[p, g]) >= 10]
            a[p, g + 8] = far[np.random.randint(len(far))]
    return np.exp2(a.ravel()).repeat(32)


BF16 = ml_dtypes.bfloat16


def bf(x):
    return np.asarray(x, np.float32).astype(BF16)


def f64(x):
    return np.asarray(x).astype(np.float64)


B, L, E, H, C, EO = 1, 1024, 2048, 16, 512, 2048
EPS = 1e-8


def sigmoid(v):
    return 1.0 / (1.0 + np.exp(-v))


def setup_inputs():
    s = mx_kscale(E)
    return {"o_attn": bf(np.random.standard_normal((L, B, E)) * 2.0),
            "Wo": bf(np.random.standard_normal((EO, E)) / np.sqrt(E) / s),
            "bo": bf(np.random.standard_normal(EO) * 0.1),
            "norm_scale": bf((1.0 + 0.1 * np.random.standard_normal(E)) * s),
            "norm_gate": bf(1.0 + 0.1 * np.random.standard_normal(E))}


def reference(o_attn, Wo, bo, norm_scale, norm_gate):
    o = f64(o_attn)
    rms = np.sqrt(np.sum(o * o, -1, keepdims=True)) * E ** -0.5
    y = f64(norm_scale) * (o / (rms + EPS)) * sigmoid(f64(norm_gate) * o)
    return (mxq(y, 2, "e4m3") @ mxq(f64(Wo), 1, "e4m3").T) + f64(bo)

@@ -1,0 +1,351 @@
+from contextlib import ExitStack
+
+import concourse.mybir as mybir
+from concourse.masks import make_identity
+
+F32 = mybir.dt.float32
+BF16 = mybir.dt.bfloat16
+U32 = mybir.dt.uint32
+U8 = mybir.dt.uint8
+FP8X4 = mybir.dt.float8_e4m3fn_x4
+ACT = mybir.ActivationFunctionType
+ALU = mybir.AluOpType
+
+P = 128
+L = 1024
+K = 2048
+N = 2048
+EPS = 1e-8
+
+PACK = 4
+K_PASS = P * PACK
+PASSES = K // K_PASS
+PAIR = 2
+HALVES = PACK // PAIR
+PASS_WORDS = K_PASS // PAIR
+
+L_GROUP = 256
+L_TILES = L_GROUP // P
+GROUPS = L // L_GROUP
+N_CHUNK = 512
+CHUNKS = N // N_CHUNK
+N_LOAD = 256
+N_TILES = N_LOAD // P
+LOADS_PER_CHUNK = N_CHUNK // N_LOAD
+
+SLOTS = GROUPS * PASSES
+PIECES = PASSES
+PIECE_K = L_TILES * K // PIECES
+TILES_PER_SLOT = 3
+G_ROWS = 128
+
+FLOPS = 2 * L * K * N
+
+
+def tile_normlocalattention_pb_kernel(tc, o_attn, Wo, bo, norm_scale, norm_gate, out):
+    nc = tc.nc
+    o_rows = o_attn.flatten_outer_dims()
+    out_rows = out.flatten_outer_dims()
+
+    with ExitStack() as stack:
+        stack.enter_context(tc.manual_schedule())
+        keep = stack.enter_context(tc.tile_pool(name="keep", bufs=1))
+        small = stack.enter_context(tc.tile_pool(name="small", bufs=2))
+        three = stack.enter_context(tc.tile_pool(name="three", bufs=3))
+        one = stack.enter_context(tc.tile_pool(name="one", bufs=1))
+        two = stack.enter_context(tc.tile_pool(name="two", bufs=2))
+        four = stack.enter_context(tc.tile_pool(name="four", bufs=4))
+        results = stack.enter_context(tc.tile_pool(name="results", bufs=4))
+        y_banks = stack.enter_context(tc.psum_pool(name="y_banks", bufs=2))
+        w_banks = stack.enter_context(tc.psum_pool(name="w_banks", bufs=2))
+        sums = stack.enter_context(tc.psum_pool(name="sums", bufs=4))
+
+        ident = keep.tile([P, P], F32)
+        make_identity(nc, ident[:])
+        half = keep.tile([P, L_TILES], F32)
+        nc.vector.memset(half[:], 0.5)
+        vec_rows = keep.tile([P, K_PASS], BF16)
+        nc.vector.memset(vec_rows[:], 0.0)
+
+        nc.sync.dma_start(out=vec_rows[0:PASSES, :], in_=norm_gate.rearrange("(b c) -> b c", c=K_PASS))
+        nc.sync.dma_start(
+            out=vec_rows[PASSES : 2 * PASSES, :], in_=norm_scale.rearrange("(b c) -> b c", c=K_PASS)
+        )
+        o_sb = [keep.tile([P, L_TILES, K], BF16, name="o_sb%d" % j) for j in range(GROUPS)]
+        w_sb = [keep.tile([P, N_TILES, K], BF16, name="w_sb%d" % h) for h in range(N // N_LOAD)]
+        bias = keep.tile([P, N], BF16)
+
+        def load_o(j):
+            rows = o_rows[j * L_GROUP : (j + 1) * L_GROUP, :]
+            nc.sync.dma_start(out=o_sb[j][:], in_=rows.rearrange("(i p) k -> p i k", p=P))
+
+        def load_w(c):
+            for h in range(c * LOADS_PER_CHUNK, (c + 1) * LOADS_PER_CHUNK):
+                rows = Wo[h * N_LOAD : (h + 1) * N_LOAD, :]
+                nc.sync.dma_start(out=w_sb[h][:], in_=rows.rearrange("(i p) k -> p i k", p=P))
+
+        load_o(0)
+        load_o(1)
+        load_w(0)
+        load_w(1)
+        nc.sync.dma_start(out=bias[:], in_=bo.partition_broadcast(P))
+        load_o(2)
+        load_w(2)
+        load_o(3)
+        load_w(3)
+
+        vec_t = sums.tile([P, N_CHUNK], F32, tag="sum")
+        for u in range(HALVES):
+            nc.tensor.transpose(
+                vec_t[:, u * P : (u + 1) * P], vec_rows[:].bitcast(F32)[:, u:PASS_WORDS:HALVES], ident[:]
+            )
+        per_channel = keep.tile([P, HALVES, 2 * PASSES * PAIR], F32)
+        for u in range(HALVES):
+            nc.vector.tensor_copy(
+                out=per_channel[:, u, :], in_=vec_t[:, u * P : u * P + 2 * PASSES].bitcast(BF16)
+            )
+
+        def gate_of(g, u, e):
+            col = g * PAIR + e
+            return per_channel[:, u, col : col + 1]
+
+        def scale_of(g, u, e):
+            col = (PASSES + g) * PAIR + e
+            return per_channel[:, u, col : col + 1]
+
+        y_codes = keep.tile([P, PASSES, L], U32, align_bytes=64)
+        y_scales = keep.tile([P, PASSES, L], U8, align_bytes=64)
+        w_codes = keep.tile([P, PASSES, N], U32, align_bytes=64)
+        w_scales = keep.tile([P, PASSES, N], U8, align_bytes=64)
+        inv_r = keep.tile([P, L], F32)
+        sum_sq = [keep.tile([P, L_TILES, PIECES // L_TILES], F32, name="sum_sq%d" % j) for j in range(GROUPS)]
+
+        y_bank, gated_of, scaled_of, y_bf_of = {}, {}, {}, {}
+        w_bank, w_bf_of = {}, {}
+        repeated_of, spread_of, sum_of = {}, {}, {}
+
+        def flip_words(bank, rows_sb, g):
+            for u in range(HALVES):
+                words = slice(g * PASS_WORDS + u, (g + 1) * PASS_WORDS, HALVES)
+                for i in range(N_TILES):
+                    nc.tensor.transpose(
+                        bank[:, u, i * P : (i + 1) * P],
+                        rows_sb[:, i, :].bitcast(F32)[:, words],
+                        ident[:],
+                    )
+
+        def squares(j, q):
+            i, part = divmod(q, PIECES // L_TILES)
+            junk = two.tile([P, PIECE_K], BF16)
+            nc.scalar.activation(
+                out=junk[:],
+                in_=o_sb[j][:, i, part * PIECE_K : (part + 1) * PIECE_K],
+                func=ACT.Square,
+                accum_out=sum_sq[j][:, i, part : part + 1],
+            )
+
+        def norms(j):
+            total = small.tile([P, L_TILES], F32)
+            nc.gpsimd.tensor_tensor(out=total[:], in0=sum_sq[j][:, :, 0], in1=sum_sq[j][:, :, 1], op=ALU.add)
+            root = small.tile([P, L_TILES], F32)
+            nc.gpsimd.tensor_tensor(out=root[:], in0=total[:], in1=half[:], op=ALU.pow)
+            r_eps = small.tile([P, L_TILES], F32)
+            nc.vector.tensor_scalar(
+                out=r_eps[:], in0=root[:], scalar1=K**-0.5, scalar2=EPS, op0=ALU.mult, op1=ALU.add
+            )
+            inv = small.tile([P, L_TILES], F32)
+            nc.vector.reciprocal(out=inv[:], in_=r_eps[:])
+            repeated = small.tile([P, L_TILES, P], F32)
+            nc.vector.tensor_copy(out=repeated[:], in_=inv[:].unsqueeze(2).to_broadcast([P, L_TILES, P]))
+            repeated_of[j] = repeated
+
+        def spread_norms(j):
+            spread = sums.tile([P, N_CHUNK], F32, tag="sum")
+            for i in range(L_TILES):
+                nc.tensor.transpose(spread[:, i * P : (i + 1) * P], repeated_of[j][:, i, :], ident[:])
+            spread_of[j] = spread
+
+        def keep_norms(j):
+            nc.vector.tensor_copy(out=inv_r[:, j * L_GROUP : (j + 1) * L_GROUP], in_=spread_of[j][:, 0:L_GROUP])
+
+        def flip_y(s):
+            j, g = divmod(s, PASSES)
+            bank = y_banks.tile([P, HALVES, L_GROUP], F32, tag="y")
+            flip_words(bank, o_sb[j], g)
+            y_bank[s] = bank
+
+        def o_t_of(s):
+            return y_bank[s][:].bitcast(BF16).rearrange("p u (l e) -> p u l e", e=PAIR)
+
+        def gate(s):
+            g = s % PASSES
+            gated = three.tile([P, PACK, L_GROUP], F32)
+            for u in range(HALVES):
+                for e in range(PAIR):
+                    nc.scalar.activation(
+                        out=gated[:, u * PAIR + e, :],
+                        in_=o_t_of(s)[:, u, :, e],
+                        func=ACT.Sigmoid,
+                        scale=gate_of(g, u, e),
+                    )
+            gated_of[s] = gated
+
+        def weigh(s):
+            g = s % PASSES
+            scaled = three.tile([P, PACK, L_GROUP], F32)
+            for u in range(HALVES):
+                for e in range(PAIR):
+                    nc.vector.scalar_tensor_tensor(
+                        out=scaled[:, u * PAIR + e, :],
+                        in0=o_t_of(s)[:, u, :, e],
+                        scalar=scale_of(g, u, e),
+                        in1=gated_of[s][:, u * PAIR + e, :],
+                        op0=ALU.mult,
+                        op1=ALU.mult,
+                    )
+            scaled_of[s] = scaled
+
+        def normalise(engine, s, first, rows):
+            start = (s // PASSES) * L_GROUP + first
+            engine.tensor_tensor(
+                out=y_bf_of[s][:, first : first + rows, :],
+                in0=scaled_of[s][:, :, first : first + rows].rearrange("p t l -> p l t"),
+                in1=inv_r[:, start : start + rows].unsqueeze(2).to_broadcast([P, rows, PACK]),
+                op=ALU.mult,
+            )
+
+        def normalise_on_gpsimd(s):
+            y_bf = one.tile([P, L_GROUP, PACK], BF16, align_bytes=64)
+            y_bf_of[s] = y_bf
+            normalise(nc.gpsimd, s, 0, G_ROWS)
+
+        def normalise_on_vector(s):
+            normalise(nc.vector, s, G_ROWS, L_GROUP - G_ROWS)
+
+        def quantise_y(s):
+            j, g = divmod(s, PASSES)
+            cols = slice(j * L_GROUP, (j + 1) * L_GROUP)
+            nc.vector.quantize_mx(
+                out=y_codes[:, g, cols].bitcast(FP8X4),
+                scales=y_scales[:, g, cols],
+                in_=y_bf_of[s][:].rearrange("p l t -> p (l t)"),
+            )
+
+        def flip_w(s):
+            c, g = divmod(s, PASSES)
+            for h in range(LOADS_PER_CHUNK):
+                bank = w_banks.tile([P, HALVES, N_LOAD], F32, tag="w")
+                flip_words(bank, w_sb[c * LOADS_PER_CHUNK + h], g)
+                w_bank[(s, h)] = bank
+
+        def copy_w(s):
+            w_bf = four.tile([P, N_CHUNK, PACK], BF16, align_bytes=64)
+            for h in range(LOADS_PER_CHUNK):
+                nc.scalar.copy(
+                    out=w_bf[:].bitcast(F32)[:, h * N_LOAD : (h + 1) * N_LOAD, :],
+                    in_=w_bank[(s, h)][:].rearrange("p u n -> p n u"),
+                )
+            w_bf_of[s] = w_bf
+
+        def quantise_w(s):
+            c, g = divmod(s, PASSES)
+            cols = slice(c * N_CHUNK, (c + 1) * N_CHUNK)
+            nc.vector.quantize_mx(
+                out=w_codes[:, g, cols].bitcast(FP8X4),
+                scales=w_scales[:, g, cols],
+                in_=w_bf_of[s][:].rearrange("p n t -> p (n t)"),
+            )
+
+        def multiply(tile):
+            row_tile, c = tile
+            l_cols = slice(row_tile * P, (row_tile + 1) * P)
+            n_cols = slice(c * N_CHUNK, (c + 1) * N_CHUNK)
+            acc = sums.tile([P, N_CHUNK], F32, tag="sum")
+            for g in range(PASSES):
+                nc.tensor.matmul_mx(
+                    out=acc[:],
+                    lhsT=y_codes[:, g, l_cols].bitcast(FP8X4),
+                    lhsT_scale=y_scales[:, g, l_cols],
+                    rhs=w_codes[:, g, n_cols].bitcast(FP8X4),
+                    rhs_scale=w_scales[:, g, n_cols],
+                    start=(g == 0),
+                    stop=(g == PASSES - 1),
+                )
+            sum_of[tile] = acc
+
+        def add_bias(tile):
+            row_tile, c = tile
+            l_cols = slice(row_tile * P, (row_tile + 1) * P)
+            n_cols = slice(c * N_CHUNK, (c + 1) * N_CHUNK)
+            result = results.tile([P, N_CHUNK], F32)
+            nc.vector.tensor_tensor(out=result[:], in0=sum_of[tile][:], in1=bias[:, n_cols], op=ALU.add)
+            nc.sync.dma_start(out=out_rows[l_cols, n_cols], in_=result[:])
+
+        def w_units_of(s):
+            last = SLOTS - PASSES
+            if s < last:
+                return [s]
+            return [w for w in (last + 2 * (s - last), last + 2 * (s - last) + 1) if w < SLOTS]
+
+        def tiles_of(j, c):
+            return [(j * L_TILES + i, c) for i in range(L_TILES)]
+
+        for q in range(PIECES):
+            squares(0, q)
+        norms(0)
+        flip_y(0)
+
+        waiting = []
+        groups_done, chunks_done = [], []
+        for s in range(SLOTS + 1):
+            j, g = divmod(s, PASSES)
+            before = s - 1
+
+            for w in w_units_of(s)[:1]:
+                flip_w(w)
+            if s + 1 < SLOTS:
+                flip_y(s + 1)
+            if g == 0 and s < SLOTS:
+                spread_norms(j)
+            now = waiting[:TILES_PER_SLOT]
+            waiting = waiting[TILES_PER_SLOT:]
+            for tile in now:
+                multiply(tile)
+
+            if s < SLOTS:
+                gate(s)
+                if j + 1 < GROUPS:
+                    squares(j + 1, g)
+            for w in w_units_of(s)[:1]:
+                copy_w(w)
+            for w in w_units_of(s)[1:]:
+                flip_w(w)
+                copy_w(w)
+
+            if s < SLOTS:
+                weigh(s)
+            for tile in now:
+                add_bias(tile)
+            if g == 0 and s < SLOTS:
+                keep_norms(j)
+            if before >= 0:
+                normalise_on_vector(before)
+                for w in w_units_of(before):
+                    quantise_w(w)
+                    if w % PASSES == PASSES - 1:
+                        chunks_done.append(w // PASSES)
+                        for other in groups_done:
+                            waiting.extend(tiles_of(other, w // PASSES))
+                quantise_y(before)
+                if before % PASSES == PASSES - 1:
+                    groups_done.append(before // PASSES)
+                    for c in chunks_done:
+                        waiting.extend(tiles_of(before // PASSES, c))
+            if g == PASSES - 1 and j + 1 < GROUPS:
+                norms(j + 1)
+            if s < SLOTS:
+                normalise_on_gpsimd(s)
+
+        for tile in waiting:
+            multiply(tile)
+            add_bias(tile)

@@ -16,6 +16,7 @@ L = 1024
 K = 2048
 N = 2048
 EPS = 1e-8
+TINY_GATE = 2.0**-60
 
 PACK = 4
 K_PASS = P * PACK
@@ -24,20 +25,17 @@ PAIR = 2
 HALVES = PACK // PAIR
 PASS_WORDS = K_PASS // PAIR
 
-L_GROUP = 256
-L_TILES = L_GROUP // P
-GROUPS = L // L_GROUP
+ROWS = 256
+TILES = ROWS // P
+GROUPS = L // ROWS
+LOADS = N // ROWS
 N_CHUNK = 512
 CHUNKS = N // N_CHUNK
-N_LOAD = 256
-N_TILES = N_LOAD // P
-LOADS_PER_CHUNK = N_CHUNK // N_LOAD
+LOADS_PER_CHUNK = N_CHUNK // ROWS
 
-SLOTS = GROUPS * PASSES
+UNITS = GROUPS * PASSES
 PIECES = PASSES
-PIECE_K = L_TILES * K // PIECES
-TILES_PER_SLOT = 3
-G_ROWS = 128
+PIECE_K = TILES * K // PIECES
 
 FLOPS = 2 * L * K * N
 
@@ -51,19 +49,19 @@ def tile_normlocalattention_pb_kernel(tc, o_attn, Wo, bo, norm_scale, norm_gate,
         stack.enter_context(tc.manual_schedule())
         keep = stack.enter_context(tc.tile_pool(name="keep", bufs=1))
         small = stack.enter_context(tc.tile_pool(name="small", bufs=2))
-        three = stack.enter_context(tc.tile_pool(name="three", bufs=3))
-        one = stack.enter_context(tc.tile_pool(name="one", bufs=1))
-        two = stack.enter_context(tc.tile_pool(name="two", bufs=2))
-        four = stack.enter_context(tc.tile_pool(name="four", bufs=4))
-        results = stack.enter_context(tc.tile_pool(name="results", bufs=4))
+        y_work = stack.enter_context(tc.tile_pool(name="y_work", bufs=4))
+        w_work = stack.enter_context(tc.tile_pool(name="w_work", bufs=8))
+        results = stack.enter_context(tc.tile_pool(name="results", bufs=6))
+        spreads = stack.enter_context(tc.psum_pool(name="spreads", bufs=1))
         y_banks = stack.enter_context(tc.psum_pool(name="y_banks", bufs=2))
-        w_banks = stack.enter_context(tc.psum_pool(name="w_banks", bufs=2))
-        sums = stack.enter_context(tc.psum_pool(name="sums", bufs=4))
+        banks = stack.enter_context(tc.psum_pool(name="banks", bufs=5))
 
         ident = keep.tile([P, P], F32)
         make_identity(nc, ident[:])
-        half = keep.tile([P, L_TILES], F32)
+        half = keep.tile([P, TILES], F32)
         nc.vector.memset(half[:], 0.5)
+        minus_one = keep.tile([P, TILES], F32)
+        nc.vector.memset(minus_one[:], -1.0)
         vec_rows = keep.tile([P, K_PASS], BF16)
         nc.vector.memset(vec_rows[:], 0.0)
 
@@ -71,63 +69,74 @@ def tile_normlocalattention_pb_kernel(tc, o_attn, Wo, bo, norm_scale, norm_gate,
         nc.sync.dma_start(
             out=vec_rows[PASSES : 2 * PASSES, :], in_=norm_scale.rearrange("(b c) -> b c", c=K_PASS)
         )
-        o_sb = [keep.tile([P, L_TILES, K], BF16, name="o_sb%d" % j) for j in range(GROUPS)]
-        w_sb = [keep.tile([P, N_TILES, K], BF16, name="w_sb%d" % h) for h in range(N // N_LOAD)]
+        o_sb = [keep.tile([P, TILES, K], BF16, name="o_sb%d" % j) for j in range(GROUPS)]
+        w_sb = [keep.tile([P, TILES, K], BF16, name="w_sb%d" % h) for h in range(LOADS)]
         bias = keep.tile([P, N], BF16)
 
         def load_o(j):
-            rows = o_rows[j * L_GROUP : (j + 1) * L_GROUP, :]
-            nc.sync.dma_start(out=o_sb[j][:], in_=rows.rearrange("(i p) k -> p i k", p=P))
+            for i in range(TILES):
+                first = j * ROWS + i * P
+                nc.sync.dma_start(out=o_sb[j][:, i, :], in_=o_rows[first : first + P, :])
 
-        def load_w(c):
-            for h in range(c * LOADS_PER_CHUNK, (c + 1) * LOADS_PER_CHUNK):
-                rows = Wo[h * N_LOAD : (h + 1) * N_LOAD, :]
-                nc.sync.dma_start(out=w_sb[h][:], in_=rows.rearrange("(i p) k -> p i k", p=P))
+        def load_w(h):
+            rows = Wo[h * ROWS : (h + 1) * ROWS, :]
+            nc.sync.dma_start(out=w_sb[h][:], in_=rows.rearrange("(i p) k -> p i k", p=P))
 
         load_o(0)
+        for h in range(3):
+            load_w(h)
         load_o(1)
-        load_w(0)
-        load_w(1)
+        for h in range(3, 6):
+            load_w(h)
         nc.sync.dma_start(out=bias[:], in_=bo.partition_broadcast(P))
         load_o(2)
-        load_w(2)
+        for h in range(6, LOADS):
+            load_w(h)
         load_o(3)
-        load_w(3)
 
-        vec_t = sums.tile([P, N_CHUNK], F32, tag="sum")
+        vec_t = banks.tile([P, N_CHUNK], F32, tag="bank")
         for u in range(HALVES):
             nc.tensor.transpose(
                 vec_t[:, u * P : (u + 1) * P], vec_rows[:].bitcast(F32)[:, u:PASS_WORDS:HALVES], ident[:]
             )
-        per_channel = keep.tile([P, HALVES, 2 * PASSES * PAIR], F32)
+        channels = PASSES * PAIR
+        raw = keep.tile([P, HALVES, 2 * channels], F32)
         for u in range(HALVES):
             nc.vector.tensor_copy(
-                out=per_channel[:, u, :], in_=vec_t[:, u * P : u * P + 2 * PASSES].bitcast(BF16)
+                out=raw[:, u, :], in_=vec_t[:, u * P : u * P + 2 * PASSES].bitcast(BF16)
             )
-
-        def gate_of(g, u, e):
-            col = g * PAIR + e
-            return per_channel[:, u, col : col + 1]
-
-        def scale_of(g, u, e):
-            col = (PASSES + g) * PAIR + e
-            return per_channel[:, u, col : col + 1]
+        raw_gate, raw_scale = raw[:, :, 0:channels], raw[:, :, channels : 2 * channels]
+        square = keep.tile([P, HALVES, channels], F32)
+        nc.vector.tensor_tensor(out=square[:], in0=raw_gate, in1=raw_gate, op=ALU.mult)
+        filler = keep.tile([P, HALVES, channels], F32)
+        nc.vector.tensor_scalar(
+            out=filler[:], in0=square[:], scalar1=TINY_GATE**2, scalar2=TINY_GATE, op0=ALU.is_lt, op1=ALU.mult
+        )
+        kept = keep.tile([P, HALVES, channels], F32)
+        nc.vector.scalar_tensor_tensor(
+            out=kept[:], in0=square[:], scalar=TINY_GATE**2, in1=raw_gate, op0=ALU.is_ge, op1=ALU.mult
+        )
+        gates = keep.tile([P, HALVES, channels], F32)
+        nc.vector.tensor_tensor(out=gates[:], in0=kept[:], in1=filler[:], op=ALU.add)
+        inv_gate = keep.tile([P, HALVES, channels], F32)
+        nc.vector.reciprocal(out=inv_gate[:], in_=gates[:])
+        ratios = keep.tile([P, HALVES, channels], F32)
+        nc.vector.tensor_tensor(out=ratios[:], in0=raw_scale, in1=inv_gate[:], op=ALU.mult)
 
         y_codes = keep.tile([P, PASSES, L], U32, align_bytes=64)
         y_scales = keep.tile([P, PASSES, L], U8, align_bytes=64)
         w_codes = keep.tile([P, PASSES, N], U32, align_bytes=64)
         w_scales = keep.tile([P, PASSES, N], U8, align_bytes=64)
-        inv_r = keep.tile([P, L], F32)
-        sum_sq = [keep.tile([P, L_TILES, PIECES // L_TILES], F32, name="sum_sq%d" % j) for j in range(GROUPS)]
+        sum_sq = [keep.tile([P, TILES, PIECES // TILES], F32, name="sum_sq%d" % j) for j in range(GROUPS)]
 
         y_bank, gated_of, scaled_of, y_bf_of = {}, {}, {}, {}
         w_bank, w_bf_of = {}, {}
-        repeated_of, spread_of, sum_of = {}, {}, {}
+        inv_of, spread_of, sum_of = {}, {}, {}
 
         def flip_words(bank, rows_sb, g):
             for u in range(HALVES):
                 words = slice(g * PASS_WORDS + u, (g + 1) * PASS_WORDS, HALVES)
-                for i in range(N_TILES):
+                for i in range(TILES):
                     nc.tensor.transpose(
                         bank[:, u, i * P : (i + 1) * P],
                         rows_sb[:, i, :].bitcast(F32)[:, words],
@@ -135,8 +144,8 @@ def tile_normlocalattention_pb_kernel(tc, o_attn, Wo, bo, norm_scale, norm_gate,
                     )
 
         def squares(j, q):
-            i, part = divmod(q, PIECES // L_TILES)
-            junk = two.tile([P, PIECE_K], BF16)
+            i, part = divmod(q, PIECES // TILES)
+            junk = small.tile([P, PIECE_K], BF16)
             nc.scalar.activation(
                 out=junk[:],
                 in_=o_sb[j][:, i, part * PIECE_K : (part + 1) * PIECE_K],
@@ -145,122 +154,105 @@ def tile_normlocalattention_pb_kernel(tc, o_attn, Wo, bo, norm_scale, norm_gate,
             )
 
         def norms(j):
-            total = small.tile([P, L_TILES], F32)
+            total = small.tile([P, TILES], F32)
             nc.gpsimd.tensor_tensor(out=total[:], in0=sum_sq[j][:, :, 0], in1=sum_sq[j][:, :, 1], op=ALU.add)
-            root = small.tile([P, L_TILES], F32)
+            root = small.tile([P, TILES], F32)
             nc.gpsimd.tensor_tensor(out=root[:], in0=total[:], in1=half[:], op=ALU.pow)
-            r_eps = small.tile([P, L_TILES], F32)
-            nc.vector.tensor_scalar(
+            r_eps = small.tile([P, TILES], F32)
+            nc.gpsimd.tensor_scalar(
                 out=r_eps[:], in0=root[:], scalar1=K**-0.5, scalar2=EPS, op0=ALU.mult, op1=ALU.add
             )
-            inv = small.tile([P, L_TILES], F32)
-            nc.vector.reciprocal(out=inv[:], in_=r_eps[:])
-            repeated = small.tile([P, L_TILES, P], F32)
-            nc.vector.tensor_copy(out=repeated[:], in_=inv[:].unsqueeze(2).to_broadcast([P, L_TILES, P]))
-            repeated_of[j] = repeated
+            inv = small.tile([P, TILES], F32)
+            nc.gpsimd.tensor_tensor(out=inv[:], in0=r_eps[:], in1=minus_one[:], op=ALU.pow)
+            inv_of[j] = inv
 
         def spread_norms(j):
-            spread = sums.tile([P, N_CHUNK], F32, tag="sum")
-            for i in range(L_TILES):
-                nc.tensor.transpose(spread[:, i * P : (i + 1) * P], repeated_of[j][:, i, :], ident[:])
+            spread = spreads.tile([P, ROWS], F32)
+            for i in range(TILES):
+                nc.tensor.transpose(
+                    spread[:, i * P : (i + 1) * P], inv_of[j][:, i : i + 1].to_broadcast([P, P]), ident[:]
+                )
             spread_of[j] = spread
 
-        def keep_norms(j):
-            nc.vector.tensor_copy(out=inv_r[:, j * L_GROUP : (j + 1) * L_GROUP], in_=spread_of[j][:, 0:L_GROUP])
-
-        def flip_y(s):
-            j, g = divmod(s, PASSES)
-            bank = y_banks.tile([P, HALVES, L_GROUP], F32, tag="y")
+        def flip_y(n):
+            j, g = divmod(n, PASSES)
+            bank = y_banks.tile([P, HALVES, ROWS], F32, tag="y")
             flip_words(bank, o_sb[j], g)
-            y_bank[s] = bank
+            y_bank[n] = bank
 
-        def o_t_of(s):
-            return y_bank[s][:].bitcast(BF16).rearrange("p u (l e) -> p u l e", e=PAIR)
-
-        def gate(s):
-            g = s % PASSES
-            gated = three.tile([P, PACK, L_GROUP], F32)
+        def gate(n):
+            g = n % PASSES
+            o_t = y_bank[n][:].bitcast(BF16).rearrange("p u (l e) -> p u l e", e=PAIR)
+            gated = y_work.tile([P, PACK, ROWS], F32)
             for u in range(HALVES):
                 for e in range(PAIR):
+                    col = g * PAIR + e
                     nc.scalar.activation(
                         out=gated[:, u * PAIR + e, :],
-                        in_=o_t_of(s)[:, u, :, e],
-                        func=ACT.Sigmoid,
-                        scale=gate_of(g, u, e),
+                        in_=o_t[:, u, :, e],
+                        func=ACT.Silu,
+                        scale=gates[:, u, col : col + 1],
                     )
-            gated_of[s] = gated
+            gated_of[n] = gated
 
-        def weigh(s):
-            g = s % PASSES
-            scaled = three.tile([P, PACK, L_GROUP], F32)
+        def weigh(n):
+            g = n % PASSES
+            scaled = y_work.tile([P, PACK, ROWS], F32)
             for u in range(HALVES):
                 for e in range(PAIR):
-                    nc.vector.scalar_tensor_tensor(
+                    col = g * PAIR + e
+                    nc.gpsimd.tensor_scalar(
                         out=scaled[:, u * PAIR + e, :],
-                        in0=o_t_of(s)[:, u, :, e],
-                        scalar=scale_of(g, u, e),
-                        in1=gated_of[s][:, u * PAIR + e, :],
+                        in0=gated_of[n][:, u * PAIR + e, :],
+                        scalar1=ratios[:, u, col : col + 1],
+                        scalar2=0.0,
                         op0=ALU.mult,
-                        op1=ALU.mult,
+                        op1=ALU.add,
                     )
-            scaled_of[s] = scaled
+            scaled_of[n] = scaled
 
-        def normalise(engine, s, first, rows):
-            start = (s // PASSES) * L_GROUP + first
-            engine.tensor_tensor(
-                out=y_bf_of[s][:, first : first + rows, :],
-                in0=scaled_of[s][:, :, first : first + rows].rearrange("p t l -> p l t"),
-                in1=inv_r[:, start : start + rows].unsqueeze(2).to_broadcast([P, rows, PACK]),
+        def normalise(n):
+            y_bf = y_work.tile([P, ROWS, PACK], BF16, align_bytes=64)
+            nc.vector.tensor_tensor(
+                out=y_bf[:],
+                in0=scaled_of[n][:].rearrange("p t l -> p l t"),
+                in1=spread_of[n // PASSES][:].unsqueeze(2).to_broadcast([P, ROWS, PACK]),
                 op=ALU.mult,
             )
+            y_bf_of[n] = y_bf
 
-        def normalise_on_gpsimd(s):
-            y_bf = one.tile([P, L_GROUP, PACK], BF16, align_bytes=64)
-            y_bf_of[s] = y_bf
-            normalise(nc.gpsimd, s, 0, G_ROWS)
-
-        def normalise_on_vector(s):
-            normalise(nc.vector, s, G_ROWS, L_GROUP - G_ROWS)
-
-        def quantise_y(s):
-            j, g = divmod(s, PASSES)
-            cols = slice(j * L_GROUP, (j + 1) * L_GROUP)
+        def quantise_y(n):
+            j, g = divmod(n, PASSES)
+            cols = slice(j * ROWS, (j + 1) * ROWS)
             nc.vector.quantize_mx(
                 out=y_codes[:, g, cols].bitcast(FP8X4),
                 scales=y_scales[:, g, cols],
-                in_=y_bf_of[s][:].rearrange("p l t -> p (l t)"),
+                in_=y_bf_of[n][:].rearrange("p l t -> p (l t)"),
             )
 
-        def flip_w(s):
-            c, g = divmod(s, PASSES)
-            for h in range(LOADS_PER_CHUNK):
-                bank = w_banks.tile([P, HALVES, N_LOAD], F32, tag="w")
-                flip_words(bank, w_sb[c * LOADS_PER_CHUNK + h], g)
-                w_bank[(s, h)] = bank
+        def flip_w(h, g):
+            bank = banks.tile([P, HALVES, ROWS], F32, tag="bank")
+            flip_words(bank, w_sb[h], g)
+            w_bank[(h, g)] = bank
 
-        def copy_w(s):
-            w_bf = four.tile([P, N_CHUNK, PACK], BF16, align_bytes=64)
-            for h in range(LOADS_PER_CHUNK):
-                nc.scalar.copy(
-                    out=w_bf[:].bitcast(F32)[:, h * N_LOAD : (h + 1) * N_LOAD, :],
-                    in_=w_bank[(s, h)][:].rearrange("p u n -> p n u"),
-                )
-            w_bf_of[s] = w_bf
+        def copy_w(copy, h, g):
+            w_bf = w_work.tile([P, ROWS, PACK], BF16, align_bytes=64)
+            copy(out=w_bf[:].bitcast(F32), in_=w_bank[(h, g)][:].rearrange("p u n -> p n u"))
+            w_bf_of[(h, g)] = w_bf
 
-        def quantise_w(s):
-            c, g = divmod(s, PASSES)
-            cols = slice(c * N_CHUNK, (c + 1) * N_CHUNK)
+        def quantise_w(h, g):
+            cols = slice(h * ROWS, (h + 1) * ROWS)
             nc.vector.quantize_mx(
                 out=w_codes[:, g, cols].bitcast(FP8X4),
                 scales=w_scales[:, g, cols],
-                in_=w_bf_of[s][:].rearrange("p n t -> p (n t)"),
+                in_=w_bf_of[(h, g)][:].rearrange("p n t -> p (n t)"),
             )
 
         def multiply(tile):
             row_tile, c = tile
             l_cols = slice(row_tile * P, (row_tile + 1) * P)
             n_cols = slice(c * N_CHUNK, (c + 1) * N_CHUNK)
-            acc = sums.tile([P, N_CHUNK], F32, tag="sum")
+            acc = banks.tile([P, N_CHUNK], F32, tag="bank")
             for g in range(PASSES):
                 nc.tensor.matmul_mx(
                     out=acc[:],
@@ -281,14 +273,17 @@ def tile_normlocalattention_pb_kernel(tc, o_attn, Wo, bo, norm_scale, norm_gate,
             nc.vector.tensor_tensor(out=result[:], in0=sum_of[tile][:], in1=bias[:, n_cols], op=ALU.add)
             nc.sync.dma_start(out=out_rows[l_cols, n_cols], in_=result[:])
 
-        def w_units_of(s):
-            last = SLOTS - PASSES
-            if s < last:
-                return [s]
-            return [w for w in (last + 2 * (s - last), last + 2 * (s - last) + 1) if w < SLOTS]
-
         def tiles_of(j, c):
-            return [(j * L_TILES + i, c) for i in range(L_TILES)]
+            return [(j * TILES + i, c) for i in range(TILES)]
+
+        def unit_of(b):
+            if 0 <= b < PASSES:
+                return b
+            return b - 2 if PASSES + 2 <= b < UNITS + 2 else None
+
+        def copier_of(b, p):
+            scalars = (0, 2) if b < 2 else (0, 2, 3)
+            return nc.scalar.copy if p in scalars else nc.vector.tensor_copy
 
         for q in range(PIECES):
             squares(0, q)
@@ -297,54 +292,54 @@ def tile_normlocalattention_pb_kernel(tc, o_attn, Wo, bo, norm_scale, norm_gate,
 
         waiting = []
         groups_done, chunks_done = [], []
-        for s in range(SLOTS + 1):
-            j, g = divmod(s, PASSES)
-            before = s - 1
+        for b in range(UNITS + 3):
+            before = b - 1
+            unit_next, unit, unit_before = [unit_of(b + x) for x in (1, 0, -1)]
 
-            for w in w_units_of(s)[:1]:
-                flip_w(w)
-            if s + 1 < SLOTS:
-                flip_y(s + 1)
-            if g == 0 and s < SLOTS:
-                spread_norms(j)
-            now = waiting[:TILES_PER_SLOT]
-            waiting = waiting[TILES_PER_SLOT:]
+            if unit_next is not None:
+                flip_y(unit_next)
+            if unit is not None:
+                gate(unit)
+                weigh(unit)
+            if b < LOADS:
+                for p in range(PASSES):
+                    flip_w(b, p)
+                for p in range(PASSES):
+                    copy_w(copier_of(b, p), b, p)
+
+            take = 1 if b < LOADS else 2
+            now = waiting[:take]
+            waiting = waiting[take:]
             for tile in now:
                 multiply(tile)
+            if unit is not None and unit % PASSES == 0:
+                spread_norms(unit // PASSES)
 
-            if s < SLOTS:
-                gate(s)
-                if j + 1 < GROUPS:
-                    squares(j + 1, g)
-            for w in w_units_of(s)[:1]:
-                copy_w(w)
-            for w in w_units_of(s)[1:]:
-                flip_w(w)
-                copy_w(w)
+            if 2 <= b < UNITS - 2:
+                j, q = divmod(b + 2, PASSES)
+                squares(j, q)
+                if q == PIECES - 1:
+                    norms(j)
 
-            if s < SLOTS:
-                weigh(s)
-            for tile in now:
+            if 0 <= before < LOADS:
+                for p in range(PASSES):
+                    quantise_w(before, p)
+                if before % LOADS_PER_CHUNK == LOADS_PER_CHUNK - 1:
+                    chunks_done.append(before // LOADS_PER_CHUNK)
+                    for other in groups_done:
+                        waiting.extend(tiles_of(other, before // LOADS_PER_CHUNK))
+            for tile in now[:1]:
                 add_bias(tile)
-            if g == 0 and s < SLOTS:
-                keep_norms(j)
-            if before >= 0:
-                normalise_on_vector(before)
-                for w in w_units_of(before):
-                    quantise_w(w)
-                    if w % PASSES == PASSES - 1:
-                        chunks_done.append(w // PASSES)
-                        for other in groups_done:
-                            waiting.extend(tiles_of(other, w // PASSES))
-                quantise_y(before)
-                if before % PASSES == PASSES - 1:
-                    groups_done.append(before // PASSES)
+            if unit_before is not None:
+                quantise_y(unit_before)
+                if unit_before % PASSES == PASSES - 1:
+                    groups_done.append(unit_before // PASSES)
                     for c in chunks_done:
-                        waiting.extend(tiles_of(before // PASSES, c))
-            if g == PASSES - 1 and j + 1 < GROUPS:
-                norms(j + 1)
-            if s < SLOTS:
-                normalise_on_gpsimd(s)
+                        waiting.extend(tiles_of(unit_before // PASSES, c))
+            for tile in now[1:]:
+                add_bias(tile)
+            if unit is not None:
+                normalise(unit)
 
         for tile in waiting:
             multiply(tile)

@@ -60,6 +60,8 @@ def tile_normlocalattention_pb_kernel(tc, o_attn, Wo, bo, norm_scale, norm_gate,
         make_identity(nc, ident[:])
         half = keep.tile([P, TILES], F32)
         nc.vector.memset(half[:], 0.5)
+        warm = keep.tile([P, 1], F32)
+        nc.scalar.activation(out=warm[:], in_=half[:, 0:1], func=ACT.Silu)
         minus_one = keep.tile([P, TILES], F32)
         nc.vector.memset(minus_one[:], -1.0)
         vec_rows = keep.tile([P, K_PASS], BF16)
@@ -282,7 +284,7 @@ def tile_normlocalattention_pb_kernel(tc, o_attn, Wo, bo, norm_scale, norm_gate,
             return b - 2 if PASSES + 2 <= b < UNITS + 2 else None
 
         def copier_of(b, p):
-            scalars = (0, 2) if b < 2 else (0, 2, 3)
+            scalars = (0, 2) if b < 2 else (0, 1, 2, 3)
             return nc.scalar.copy if p in scalars else nc.vector.tensor_copy
 
         for q in range(PIECES):

from contextlib import ExitStack

import concourse.mybir as mybir
from concourse.masks import make_identity

F32 = mybir.dt.float32
BF16 = mybir.dt.bfloat16
U32 = mybir.dt.uint32
U8 = mybir.dt.uint8
FP8X4 = mybir.dt.float8_e4m3fn_x4
ACT = mybir.ActivationFunctionType
ALU = mybir.AluOpType

P = 128
L = 1024
K = 2048
N = 2048
EPS = 1e-8
TINY_GATE = 2.0**-60

PACK = 4
K_PASS = P * PACK
PASSES = K // K_PASS
PAIR = 2
HALVES = PACK // PAIR
PASS_WORDS = K_PASS // PAIR

ROWS = 256
TILES = ROWS // P
GROUPS = L // ROWS
LOADS = N // ROWS
N_CHUNK = 512
CHUNKS = N // N_CHUNK
LOADS_PER_CHUNK = N_CHUNK // ROWS

UNITS = GROUPS * PASSES
PIECES = PASSES
PIECE_K = TILES * K // PIECES

FLOPS = 2 * L * K * N


def tile_normlocalattention_pb_kernel(tc, o_attn, Wo, bo, norm_scale, norm_gate, out):
    nc = tc.nc
    o_rows = o_attn.flatten_outer_dims()
    out_rows = out.flatten_outer_dims()

    with ExitStack() as stack:
        stack.enter_context(tc.manual_schedule())
        keep = stack.enter_context(tc.tile_pool(name="keep", bufs=1))
        small = stack.enter_context(tc.tile_pool(name="small", bufs=2))
        y_work = stack.enter_context(tc.tile_pool(name="y_work", bufs=4))
        w_work = stack.enter_context(tc.tile_pool(name="w_work", bufs=8))
        results = stack.enter_context(tc.tile_pool(name="results", bufs=6))
        spreads = stack.enter_context(tc.psum_pool(name="spreads", bufs=1))
        y_banks = stack.enter_context(tc.psum_pool(name="y_banks", bufs=2))
        banks = stack.enter_context(tc.psum_pool(name="banks", bufs=5))

        ident = keep.tile([P, P], F32)
        make_identity(nc, ident[:])
        half = keep.tile([P, TILES], F32)
        nc.vector.memset(half[:], 0.5)
        warm = keep.tile([P, 1], F32)
        nc.scalar.activation(out=warm[:], in_=half[:, 0:1], func=ACT.Silu)
        minus_one = keep.tile([P, TILES], F32)
        nc.vector.memset(minus_one[:], -1.0)
        vec_rows = keep.tile([P, K_PASS], BF16)
        nc.vector.memset(vec_rows[:], 0.0)

        nc.sync.dma_start(out=vec_rows[0:PASSES, :], in_=norm_gate.rearrange("(b c) -> b c", c=K_PASS))
        nc.sync.dma_start(
            out=vec_rows[PASSES : 2 * PASSES, :], in_=norm_scale.rearrange("(b c) -> b c", c=K_PASS)
        )
        o_sb = [keep.tile([P, TILES, K], BF16, name="o_sb%d" % j) for j in range(GROUPS)]
        w_sb = [keep.tile([P, TILES, K], BF16, name="w_sb%d" % h) for h in range(LOADS)]
        bias = keep.tile([P, N], BF16)

        def load_o(j):
            for i in range(TILES):
                first = j * ROWS + i * P
                nc.sync.dma_start(out=o_sb[j][:, i, :], in_=o_rows[first : first + P, :])

        def load_w(h):
            rows = Wo[h * ROWS : (h + 1) * ROWS, :]
            nc.sync.dma_start(out=w_sb[h][:], in_=rows.rearrange("(i p) k -> p i k", p=P))

        load_o(0)
        for h in range(3):
            load_w(h)
        load_o(1)
        for h in range(3, 6):
            load_w(h)
        nc.sync.dma_start(out=bias[:], in_=bo.partition_broadcast(P))
        load_o(2)
        for h in range(6, LOADS):
            load_w(h)
        load_o(3)

        vec_t = banks.tile([P, N_CHUNK], F32, tag="bank")
        for u in range(HALVES):
            nc.tensor.transpose(
                vec_t[:, u * P : (u + 1) * P], vec_rows[:].bitcast(F32)[:, u:PASS_WORDS:HALVES], ident[:]
            )
        channels = PASSES * PAIR
        raw = keep.tile([P, HALVES, 2 * channels], F32)
        for u in range(HALVES):
            nc.vector.tensor_copy(
                out=raw[:, u, :], in_=vec_t[:, u * P : u * P + 2 * PASSES].bitcast(BF16)
            )
        raw_gate, raw_scale = raw[:, :, 0:channels], raw[:, :, channels : 2 * channels]
        square = keep.tile([P, HALVES, channels], F32)
        nc.vector.tensor_tensor(out=square[:], in0=raw_gate, in1=raw_gate, op=ALU.mult)
        filler = keep.tile([P, HALVES, channels], F32)
        nc.vector.tensor_scalar(
            out=filler[:], in0=square[:], scalar1=TINY_GATE**2, scalar2=TINY_GATE, op0=ALU.is_lt, op1=ALU.mult
        )
        kept = keep.tile([P, HALVES, channels], F32)
        nc.vector.scalar_tensor_tensor(
            out=kept[:], in0=square[:], scalar=TINY_GATE**2, in1=raw_gate, op0=ALU.is_ge, op1=ALU.mult
        )
        gates = keep.tile([P, HALVES, channels], F32)
        nc.vector.tensor_tensor(out=gates[:], in0=kept[:], in1=filler[:], op=ALU.add)
        inv_gate = keep.tile([P, HALVES, channels], F32)
        nc.vector.reciprocal(out=inv_gate[:], in_=gates[:])
        ratios = keep.tile([P, HALVES, channels], F32)
        nc.vector.tensor_tensor(out=ratios[:], in0=raw_scale, in1=inv_gate[:], op=ALU.mult)

        y_codes = keep.tile([P, PASSES, L], U32, align_bytes=64)
        y_scales = keep.tile([P, PASSES, L], U8, align_bytes=64)
        w_codes = keep.tile([P, PASSES, N], U32, align_bytes=64)
        w_scales = keep.tile([P, PASSES, N], U8, align_bytes=64)
        sum_sq = [keep.tile([P, TILES, PIECES // TILES], F32, name="sum_sq%d" % j) for j in range(GROUPS)]

        y_bank, gated_of, scaled_of, y_bf_of = {}, {}, {}, {}
        w_bank, w_bf_of = {}, {}
        inv_of, spread_of, sum_of = {}, {}, {}

        def flip_words(bank, rows_sb, g):
            for u in range(HALVES):
                words = slice(g * PASS_WORDS + u, (g + 1) * PASS_WORDS, HALVES)
                for i in range(TILES):
                    nc.tensor.transpose(
                        bank[:, u, i * P : (i + 1) * P],
                        rows_sb[:, i, :].bitcast(F32)[:, words],
                        ident[:],
                    )

        def squares(j, q):
            i, part = divmod(q, PIECES // TILES)
            junk = small.tile([P, PIECE_K], BF16)
            nc.scalar.activation(
                out=junk[:],
                in_=o_sb[j][:, i, part * PIECE_K : (part + 1) * PIECE_K],
                func=ACT.Square,
                accum_out=sum_sq[j][:, i, part : part + 1],
            )

        def norms(j):
            total = small.tile([P, TILES], F32)
            nc.gpsimd.tensor_tensor(out=total[:], in0=sum_sq[j][:, :, 0], in1=sum_sq[j][:, :, 1], op=ALU.add)
            root = small.tile([P, TILES], F32)
            nc.gpsimd.tensor_tensor(out=root[:], in0=total[:], in1=half[:], op=ALU.pow)
            r_eps = small.tile([P, TILES], F32)
            nc.gpsimd.tensor_scalar(
                out=r_eps[:], in0=root[:], scalar1=K**-0.5, scalar2=EPS, op0=ALU.mult, op1=ALU.add
            )
            inv = small.tile([P, TILES], F32)
            nc.gpsimd.tensor_tensor(out=inv[:], in0=r_eps[:], in1=minus_one[:], op=ALU.pow)
            inv_of[j] = inv

        def spread_norms(j):
            spread = spreads.tile([P, ROWS], F32)
            for i in range(TILES):
                nc.tensor.transpose(
                    spread[:, i * P : (i + 1) * P], inv_of[j][:, i : i + 1].to_broadcast([P, P]), ident[:]
                )
            spread_of[j] = spread

        def flip_y(n):
            j, g = divmod(n, PASSES)
            bank = y_banks.tile([P, HALVES, ROWS], F32, tag="y")
            flip_words(bank, o_sb[j], g)
            y_bank[n] = bank

        def gate(n):
            g = n % PASSES
            o_t = y_bank[n][:].bitcast(BF16).rearrange("p u (l e) -> p u l e", e=PAIR)
            gated = y_work.tile([P, PACK, ROWS], F32)
            for u in range(HALVES):
                for e in range(PAIR):
                    col = g * PAIR + e
                    nc.scalar.activation(
                        out=gated[:, u * PAIR + e, :],
                        in_=o_t[:, u, :, e],
                        func=ACT.Silu,
                        scale=gates[:, u, col : col + 1],
                    )
            gated_of[n] = gated

        def weigh(n):
            g = n % PASSES
            scaled = y_work.tile([P, PACK, ROWS], F32)
            for u in range(HALVES):
                for e in range(PAIR):
                    col = g * PAIR + e
                    nc.gpsimd.tensor_scalar(
                        out=scaled[:, u * PAIR + e, :],
                        in0=gated_of[n][:, u * PAIR + e, :],
                        scalar1=ratios[:, u, col : col + 1],
                        scalar2=0.0,
                        op0=ALU.mult,
                        op1=ALU.add,
                    )
            scaled_of[n] = scaled

        def normalise(n):
            y_bf = y_work.tile([P, ROWS, PACK], BF16, align_bytes=64)
            nc.vector.tensor_tensor(
                out=y_bf[:],
                in0=scaled_of[n][:].rearrange("p t l -> p l t"),
                in1=spread_of[n // PASSES][:].unsqueeze(2).to_broadcast([P, ROWS, PACK]),
                op=ALU.mult,
            )
            y_bf_of[n] = y_bf

        def quantise_y(n):
            j, g = divmod(n, PASSES)
            cols = slice(j * ROWS, (j + 1) * ROWS)
            nc.vector.quantize_mx(
                out=y_codes[:, g, cols].bitcast(FP8X4),
                scales=y_scales[:, g, cols],
                in_=y_bf_of[n][:].rearrange("p l t -> p (l t)"),
            )

        def flip_w(h, g):
            bank = banks.tile([P, HALVES, ROWS], F32, tag="bank")
            flip_words(bank, w_sb[h], g)
            w_bank[(h, g)] = bank

        def copy_w(copy, h, g):
            w_bf = w_work.tile([P, ROWS, PACK], BF16, align_bytes=64)
            copy(out=w_bf[:].bitcast(F32), in_=w_bank[(h, g)][:].rearrange("p u n -> p n u"))
            w_bf_of[(h, g)] = w_bf

        def quantise_w(h, g):
            cols = slice(h * ROWS, (h + 1) * ROWS)
            nc.vector.quantize_mx(
                out=w_codes[:, g, cols].bitcast(FP8X4),
                scales=w_scales[:, g, cols],
                in_=w_bf_of[(h, g)][:].rearrange("p n t -> p (n t)"),
            )

        def multiply(tile):
            row_tile, c = tile
            l_cols = slice(row_tile * P, (row_tile + 1) * P)
            n_cols = slice(c * N_CHUNK, (c + 1) * N_CHUNK)
            acc = banks.tile([P, N_CHUNK], F32, tag="bank")
            for g in range(PASSES):
                nc.tensor.matmul_mx(
                    out=acc[:],
                    lhsT=y_codes[:, g, l_cols].bitcast(FP8X4),
                    lhsT_scale=y_scales[:, g, l_cols],
                    rhs=w_codes[:, g, n_cols].bitcast(FP8X4),
                    rhs_scale=w_scales[:, g, n_cols],
                    start=(g == 0),
                    stop=(g == PASSES - 1),
                )
            sum_of[tile] = acc

        def add_bias(tile):
            row_tile, c = tile
            l_cols = slice(row_tile * P, (row_tile + 1) * P)
            n_cols = slice(c * N_CHUNK, (c + 1) * N_CHUNK)
            result = results.tile([P, N_CHUNK], F32)
            nc.vector.tensor_tensor(out=result[:], in0=sum_of[tile][:], in1=bias[:, n_cols], op=ALU.add)
            nc.sync.dma_start(out=out_rows[l_cols, n_cols], in_=result[:])

        def tiles_of(j, c):
            return [(j * TILES + i, c) for i in range(TILES)]

        def unit_of(b):
            if 0 <= b < PASSES:
                return b
            return b - 2 if PASSES + 2 <= b < UNITS + 2 else None

        def copier_of(b, p):
            scalars = (0, 2) if b < 2 else (0, 1, 2, 3)
            return nc.scalar.copy if p in scalars else nc.vector.tensor_copy

        for q in range(PIECES):
            squares(0, q)
        norms(0)
        flip_y(0)

        waiting = []
        groups_done, chunks_done = [], []
        for b in range(UNITS + 3):
            before = b - 1
            unit_next, unit, unit_before = [unit_of(b + x) for x in (1, 0, -1)]

            if unit_next is not None:
                flip_y(unit_next)
            if unit is not None:
                gate(unit)
                weigh(unit)
            if b < LOADS:
                for p in range(PASSES):
                    flip_w(b, p)
                for p in range(PASSES):
                    copy_w(copier_of(b, p), b, p)

            take = 1 if b < LOADS else 2
            now = waiting[:take]
            waiting = waiting[take:]
            for tile in now:
                multiply(tile)
            if unit is not None and unit % PASSES == 0:
                spread_norms(unit // PASSES)

            if 2 <= b < UNITS - 2:
                j, q = divmod(b + 2, PASSES)
                squares(j, q)
                if q == PIECES - 1:
                    norms(j)

            if 0 <= before < LOADS:
                for p in range(PASSES):
                    quantise_w(before, p)
                if before % LOADS_PER_CHUNK == LOADS_PER_CHUNK - 1:
                    chunks_done.append(before // LOADS_PER_CHUNK)
                    for other in groups_done:
                        waiting.extend(tiles_of(other, before // LOADS_PER_CHUNK))
            for tile in now[:1]:
                add_bias(tile)
            if unit_before is not None:
                quantise_y(unit_before)
                if unit_before % PASSES == PASSES - 1:
                    groups_done.append(unit_before // PASSES)
                    for c in chunks_done:
                        waiting.extend(tiles_of(unit_before // PASSES, c))
            for tile in now[1:]:
                add_bias(tile)
            if unit is not None:
                normalise(unit)

        for tile in waiting:
            multiply(tile)
            add_bias(tile)
